import numpy as np
import ml_dtypes

BF16 = ml_dtypes.bfloat16


def bf(x):
    return np.asarray(x, np.float32).astype(BF16)


def f32(x):
    return np.asarray(x, np.float32)


def f64(x):
    return np.asarray(x).astype(np.float64)


def striped(idx):
    return np.tile(idx.reshape(-1, 16).T, (8, 1))


D, S, M, N = 128, 4096, 128, 1024
MAGS = (np.arange(D) + 1.0) / (4.0 * D)
R = float(np.sum(MAGS ** 2))


def setup_inputs():
    order = np.stack([np.random.permutation(D) for _ in range(S)], axis=1)
    signs = np.where(np.random.random((D, S)) < 0.5, -1.0, 1.0)
    return {"table": bf(MAGS[order] * signs), "w": bf(0.1 * np.random.standard_normal((D, M))), "offs": striped(np.random.permutation(np.tile(np.arange(S), 2))[:N])}


def reference(table, w, offs):
    idx = offs[:16].T.reshape(-1)
    dots = f64(w).T @ f64(table)[:, idx]
    qn = np.sqrt(np.sum(f64(w) ** 2, axis=0))[:, None]
    return dots / (qn * np.sqrt(R))

@@ -1,0 +1,47 @@
+import concourse.mybir as mybir
+
+BF16, F32, U16 = mybir.dt.bfloat16, mybir.dt.float32, mybir.dt.uint16
+
+D = 128
+S = 4096
+M = 128
+N = 1024
+R = 2.697998046875
+PIECE = 512
+
+FLOPS = 2 * D * M * N
+
+
+def tile_drmm_class_kernel(tc, table, w, offs, out):
+    nc = tc.nc
+    with (
+        tc.tile_pool(name="held", bufs=1) as held,
+        tc.tile_pool(name="work", bufs=2) as work,
+        tc.psum_pool(name="psum", bufs=1) as psum,
+        tc.psum_pool(name="banks", bufs=2) as banks,
+    ):
+        offsets = held.tile([128, N // 16], U16, name="offsets")
+        nc.sync.dma_start(offsets[:], offs)
+        queries = held.tile([D, M], BF16, name="queries")
+        nc.scalar.dma_start(queries[:], w)
+        words = held.tile([D, S], BF16, name="words")
+        nc.sync.dma_start(words[:], table)
+
+        squares = held.tile([D, M], F32, name="squares")
+        nc.vector.tensor_tensor(squares[:], queries[:], queries[:], mybir.AluOpType.mult)
+        ones = held.tile([D, 1], F32, name="ones")
+        nc.vector.memset(ones[:], 1.0)
+        norm2 = psum.tile([M, 1], F32, name="norm2")
+        nc.tensor.matmul(norm2[:], squares[:], ones[:], start=True, stop=True)
+        length = held.tile([M, 1], F32, name="length")
+        nc.scalar.activation(length[:], norm2[:], mybir.ActivationFunctionType.Sqrt, scale=R)
+        inverse = held.tile([M, 1], F32, name="inverse")
+        nc.vector.reciprocal(inverse[:], length[:])
+
+        for p in range(N // PIECE):
+            looked_up = words[:].indirect(offsets[:, p * (PIECE // 16) : (p + 1) * (PIECE // 16)])
+            dots = banks.tile([M, PIECE], F32, name="dots")
+            nc.tensor.matmul(dots[:], queries[:], looked_up, start=True, stop=True)
+            cosines = work.tile([M, PIECE], F32, name="cosines")
+            nc.vector.tensor_scalar_mul(cosines[:], dots[:], inverse[:])
+            nc.sync.dma_start(out[:, p * PIECE : (p + 1) * PIECE], cosines[:])

@@ -23,9 +23,10 @@ def tile_drmm_class_kernel(tc, table, w, offs, out):
         offsets = held.tile([128, N // 16], U16, name="offsets")
         nc.sync.dma_start(offsets[:], offs)
         queries = held.tile([D, M], BF16, name="queries")
-        nc.scalar.dma_start(queries[:], w)
+        nc.gpsimd.dma_start(queries[:], w)
         words = held.tile([D, S], BF16, name="words")
-        nc.sync.dma_start(words[:], table)
+        nc.sync.dma_start(words[:, : S // 2], table[:, : S // 2])
+        nc.scalar.dma_start(words[:, S // 2 :], table[:, S // 2 :])
 
         squares = held.tile([D, M], F32, name="squares")
         nc.vector.tensor_tensor(squares[:], queries[:], queries[:], mybir.AluOpType.mult)

@@ -7,7 +7,7 @@ S = 4096
 M = 128
 N = 1024
 R = 2.697998046875
-PIECE = 512
+PIECE = 256
 
 FLOPS = 2 * D * M * N
 
@@ -16,17 +16,16 @@ def tile_drmm_class_kernel(tc, table, w, offs, out):
     nc = tc.nc
     with (
         tc.tile_pool(name="held", bufs=1) as held,
-        tc.tile_pool(name="work", bufs=2) as work,
+        tc.tile_pool(name="work", bufs=N // PIECE) as work,
         tc.psum_pool(name="psum", bufs=1) as psum,
-        tc.psum_pool(name="banks", bufs=2) as banks,
+        tc.psum_pool(name="banks", bufs=N // PIECE) as banks,
     ):
         offsets = held.tile([128, N // 16], U16, name="offsets")
         nc.sync.dma_start(offsets[:], offs)
         queries = held.tile([D, M], BF16, name="queries")
-        nc.gpsimd.dma_start(queries[:], w)
+        nc.scalar.dma_start(queries[:], w)
         words = held.tile([D, S], BF16, name="words")
-        nc.sync.dma_start(words[:, : S // 2], table[:, : S // 2])
-        nc.scalar.dma_start(words[:, S // 2 :], table[:, S // 2 :])
+        nc.sync.dma_start(words[:], table)
 
         squares = held.tile([D, M], F32, name="squares")
         nc.vector.tensor_tensor(squares[:], queries[:], queries[:], mybir.AluOpType.mult)
@@ -44,5 +43,8 @@ def tile_drmm_class_kernel(tc, table, w, offs, out):
             dots = banks.tile([M, PIECE], F32, name="dots")
             nc.tensor.matmul(dots[:], queries[:], looked_up, start=True, stop=True)
             cosines = work.tile([M, PIECE], F32, name="cosines")
-            nc.vector.tensor_scalar_mul(cosines[:], dots[:], inverse[:])
+            if p % 2 == 0:
+                nc.vector.tensor_scalar_mul(cosines[:], dots[:], inverse[:])
+            else:
+                nc.scalar.activation(cosines[:], dots[:], mybir.ActivationFunctionType.Copy, scale=inverse[:])
             nc.sync.dma_start(out[:, p * PIECE : (p + 1) * PIECE], cosines[:])

@@ -25,7 +25,8 @@ def tile_drmm_class_kernel(tc, table, w, offs, out):
         queries = held.tile([D, M], BF16, name="queries")
         nc.scalar.dma_start(queries[:], w)
         words = held.tile([D, S], BF16, name="words")
-        nc.sync.dma_start(words[:], table)
+        nc.sync.dma_start(words[:, : S // 2], table[:, : S // 2])
+        nc.scalar.dma_start(words[:, S // 2 :], table[:, S // 2 :])
 
         squares = held.tile([D, M], F32, name="squares")
         nc.vector.tensor_tensor(squares[:], queries[:], queries[:], mybir.AluOpType.mult)

@@ -25,8 +25,8 @@ def tile_drmm_class_kernel(tc, table, w, offs, out):
         queries = held.tile([D, M], BF16, name="queries")
         nc.scalar.dma_start(queries[:], w)
         words = held.tile([D, S], BF16, name="words")
-        nc.sync.dma_start(words[:, : S // 2], table[:, : S // 2])
-        nc.scalar.dma_start(words[:, S // 2 :], table[:, S // 2 :])
+        nc.sync.dma_start(words[0:D:2, :], table[0:D:2, :])
+        nc.scalar.dma_start(words[1:D:2, :], table[1:D:2, :])
 
         squares = held.tile([D, M], F32, name="squares")
         nc.vector.tensor_tensor(squares[:], queries[:], queries[:], mybir.AluOpType.mult)

@@ -7,7 +7,8 @@ S = 4096
 M = 128
 N = 1024
 R = 2.697998046875
-PIECE = 256
+PIECE = 128
+STORE = 2 * PIECE
 
 FLOPS = 2 * D * M * N
 
@@ -16,9 +17,9 @@ def tile_drmm_class_kernel(tc, table, w, offs, out):
     nc = tc.nc
     with (
         tc.tile_pool(name="held", bufs=1) as held,
-        tc.tile_pool(name="work", bufs=N // PIECE) as work,
+        tc.tile_pool(name="work", bufs=N // STORE) as work,
         tc.psum_pool(name="psum", bufs=1) as psum,
-        tc.psum_pool(name="banks", bufs=N // PIECE) as banks,
+        tc.psum_pool(name="banks", bufs=7) as banks,
     ):
         offsets = held.tile([128, N // 16], U16, name="offsets")
         nc.sync.dma_start(offsets[:], offs)
@@ -39,13 +40,16 @@ def tile_drmm_class_kernel(tc, table, w, offs, out):
         inverse = held.tile([M, 1], F32, name="inverse")
         nc.vector.reciprocal(inverse[:], length[:])
 
-        for p in range(N // PIECE):
-            looked_up = words[:].indirect(offsets[:, p * (PIECE // 16) : (p + 1) * (PIECE // 16)])
-            dots = banks.tile([M, PIECE], F32, name="dots")
-            nc.tensor.matmul(dots[:], queries[:], looked_up, start=True, stop=True)
-            cosines = work.tile([M, PIECE], F32, name="cosines")
-            if p % 2 == 0:
-                nc.vector.tensor_scalar_mul(cosines[:], dots[:], inverse[:])
-            else:
-                nc.scalar.activation(cosines[:], dots[:], mybir.ActivationFunctionType.Copy, scale=inverse[:])
-            nc.sync.dma_start(out[:, p * PIECE : (p + 1) * PIECE], cosines[:])
+        for s in range(N // STORE):
+            cosines = work.tile([M, STORE], F32, name="cosines")
+            for half in range(2):
+                p = 2 * s + half
+                looked_up = words[:].indirect(offsets[:, p * (PIECE // 16) : (p + 1) * (PIECE // 16)])
+                dots = banks.tile([M, PIECE], F32, name="dots")
+                nc.tensor.matmul(dots[:], queries[:], looked_up, start=True, stop=True)
+                scaled = cosines[:, half * PIECE : (half + 1) * PIECE]
+                if half == 0:
+                    nc.vector.tensor_scalar_mul(scaled, dots[:], inverse[:])
+                else:
+                    nc.scalar.activation(scaled, dots[:], mybir.ActivationFunctionType.Copy, scale=inverse[:])
+            nc.sync.dma_start(out[:, s * STORE : (s + 1) * STORE], cosines[:])

@@ -21,13 +21,13 @@ def tile_drmm_class_kernel(tc, table, w, offs, out):
         tc.psum_pool(name="psum", bufs=1) as psum,
         tc.psum_pool(name="banks", bufs=7) as banks,
     ):
-        offsets = held.tile([128, N // 16], U16, name="offsets")
-        nc.sync.dma_start(offsets[:], offs)
-        queries = held.tile([D, M], BF16, name="queries")
-        nc.scalar.dma_start(queries[:], w)
         words = held.tile([D, S], BF16, name="words")
         nc.sync.dma_start(words[0:D:2, :], table[0:D:2, :])
+        queries = held.tile([D, M], BF16, name="queries")
+        nc.scalar.dma_start(queries[:], w)
         nc.scalar.dma_start(words[1:D:2, :], table[1:D:2, :])
+        offsets = held.tile([128, N // 16], U16, name="offsets")
+        nc.sync.dma_start(offsets[:], offs)
 
         squares = held.tile([D, M], F32, name="squares")
         nc.vector.tensor_tensor(squares[:], queries[:], queries[:], mybir.AluOpType.mult)

@@ -48,7 +48,7 @@ def tile_drmm_class_kernel(tc, table, w, offs, out):
                 dots = banks.tile([M, PIECE], F32, name="dots")
                 nc.tensor.matmul(dots[:], queries[:], looked_up, start=True, stop=True)
                 scaled = cosines[:, half * PIECE : (half + 1) * PIECE]
-                if half == 0:
+                if s % 2 == 0:
                     nc.vector.tensor_scalar_mul(scaled, dots[:], inverse[:])
                 else:
                     nc.scalar.activation(scaled, dots[:], mybir.ActivationFunctionType.Copy, scale=inverse[:])

@@ -48,7 +48,7 @@ def tile_drmm_class_kernel(tc, table, w, offs, out):
                 dots = banks.tile([M, PIECE], F32, name="dots")
                 nc.tensor.matmul(dots[:], queries[:], looked_up, start=True, stop=True)
                 scaled = cosines[:, half * PIECE : (half + 1) * PIECE]
-                if s % 2 == 0:
+                if s in (0, N // STORE - 1):
                     nc.vector.tensor_scalar_mul(scaled, dots[:], inverse[:])
                 else:
                     nc.scalar.activation(scaled, dots[:], mybir.ActivationFunctionType.Copy, scale=inverse[:])

@@ -21,11 +21,11 @@ def tile_drmm_class_kernel(tc, table, w, offs, out):
         tc.psum_pool(name="psum", bufs=1) as psum,
         tc.psum_pool(name="banks", bufs=7) as banks,
     ):
-        words = held.tile([D, S], BF16, name="words")
-        nc.sync.dma_start(words[0:D:2, :], table[0:D:2, :])
         queries = held.tile([D, M], BF16, name="queries")
-        nc.scalar.dma_start(queries[:], w)
+        nc.sync.dma_start(queries[:], w)
+        words = held.tile([D, S], BF16, name="words")
         nc.scalar.dma_start(words[1:D:2, :], table[1:D:2, :])
+        nc.sync.dma_start(words[0:D:2, :], table[0:D:2, :])
         offsets = held.tile([128, N // 16], U16, name="offsets")
         nc.sync.dma_start(offsets[:], offs)
 

import concourse.mybir as mybir

BF16, F32, U16 = mybir.dt.bfloat16, mybir.dt.float32, mybir.dt.uint16

D = 128
S = 4096
M = 128
N = 1024
R = 2.697998046875
PIECE = 128
STORE = 2 * PIECE

FLOPS = 2 * D * M * N


def tile_drmm_class_kernel(tc, table, w, offs, out):
    nc = tc.nc
    with (
        tc.tile_pool(name="held", bufs=1) as held,
        tc.tile_pool(name="work", bufs=N // STORE) as work,
        tc.psum_pool(name="psum", bufs=1) as psum,
        tc.psum_pool(name="banks", bufs=7) as banks,
    ):
        queries = held.tile([D, M], BF16, name="queries")
        nc.sync.dma_start(queries[:], w)
        words = held.tile([D, S], BF16, name="words")
        nc.scalar.dma_start(words[1:D:2, :], table[1:D:2, :])
        nc.sync.dma_start(words[0:D:2, :], table[0:D:2, :])
        offsets = held.tile([128, N // 16], U16, name="offsets")
        nc.sync.dma_start(offsets[:], offs)

        squares = held.tile([D, M], F32, name="squares")
        nc.vector.tensor_tensor(squares[:], queries[:], queries[:], mybir.AluOpType.mult)
        ones = held.tile([D, 1], F32, name="ones")
        nc.vector.memset(ones[:], 1.0)
        norm2 = psum.tile([M, 1], F32, name="norm2")
        nc.tensor.matmul(norm2[:], squares[:], ones[:], start=True, stop=True)
        length = held.tile([M, 1], F32, name="length")
        nc.scalar.activation(length[:], norm2[:], mybir.ActivationFunctionType.Sqrt, scale=R)
        inverse = held.tile([M, 1], F32, name="inverse")
        nc.vector.reciprocal(inverse[:], length[:])

        for s in range(N // STORE):
            cosines = work.tile([M, STORE], F32, name="cosines")
            for half in range(2):
                p = 2 * s + half
                looked_up = words[:].indirect(offsets[:, p * (PIECE // 16) : (p + 1) * (PIECE // 16)])
                dots = banks.tile([M, PIECE], F32, name="dots")
                nc.tensor.matmul(dots[:], queries[:], looked_up, start=True, stop=True)
                scaled = cosines[:, half * PIECE : (half + 1) * PIECE]
                if s in (0, N // STORE - 1):
                    nc.vector.tensor_scalar_mul(scaled, dots[:], inverse[:])
                else:
                    nc.scalar.activation(scaled, dots[:], mybir.ActivationFunctionType.Copy, scale=inverse[:])
            nc.sync.dma_start(out[:, s * STORE : (s + 1) * STORE], cosines[:])
